import numpy as np
import ml_dtypes


def mxq(x, axis, fmt="e4m3"):
    dtype, down = {"e4m3": (ml_dtypes.float8_e4m3fn, 7), "e5m2": (ml_dtypes.float8_e5m2, 14)}[fmt]
    v = np.moveaxis(np.asarray(x, np.float32).astype(ml_dtypes.bfloat16).astype(np.float64), axis, -1)
    blocks = v.reshape(v.shape[:-1] + (-1, 32))
    amax = np.abs(blocks).max(-1, keepdims=True)
    byte = np.maximum(np.where(amax > 0, np.frexp(amax)[1] - 1 + 127, 0) - down, 1)
    scale = np.exp2(byte - 127.0)
    codes = (blocks / scale).astype(np.float32).astype(dtype).astype(np.float64)
    return np.moveaxis((codes * scale).reshape(v.shape), -1, axis)


WIDE = False


def mx_kscale(k):
    if not WIDE:
        return np.ones(k)
    levels = np.array([10, -10, 5, -5, 0])
    a = np.random.permutation(np.resize(levels, k // 512 * 4)).reshape(k // 512, 4)
    idx = np.arange(k)
    return np.exp2(a[idx // 512, idx % 128 // 32])


BF16 = ml_dtypes.bfloat16


def bf(x):
    return np.asarray(x, np.float32).astype(BF16)


def f64(x):
    return np.asarray(x).astype(np.float64)


E2M1 = np.array([0.0, 0.5, 1.0, 1.5, 2.0, 3.0, 4.0, 6.0, -0.0, -0.5, -1.0, -1.5, -2.0, -3.0, -4.0, -6.0])


def pack_weight(w, fmt):
    k, n = w.shape
    w = f64(bf(w)).reshape(k // 32, 32, n)
    amax = np.abs(w).max(1)
    if fmt == "e4m3":
        byte = np.frexp(amax)[1] - 1 + 127 - 7
    else:
        mant, ex = np.frexp(amax / 6.0)
        byte = np.where(mant > 0.5, ex, ex - 1) + 127
    byte = np.clip(np.where(amax > 0, byte, 1), 1, 254)
    scaled = (w * np.exp2(127.0 - byte)[:, None, :]).reshape(k, n).astype(np.float32)
    by_word = np.ascontiguousarray(scaled.reshape(k // 512, 128, 4, n).transpose(0, 1, 3, 2))
    if fmt == "e4m3":
        words = by_word.astype(ml_dtypes.float8_e4m3fn).view(np.uint8)
    else:
        c = by_word.astype(ml_dtypes.float4_e2m1fn).view(np.uint8) & 0xF
        words = c[..., 0::2] | (c[..., 1::2] << 4)
    return np.ascontiguousarray(words), np.ascontiguousarray(byte.astype(np.uint8).reshape(k // 512, 16, n))


def unpack_weight(words, scales, fmt):
    g, p, n, _ = words.shape
    if fmt == "e4m3":
        vals = np.ascontiguousarray(words).view(ml_dtypes.float8_e4m3fn).astype(np.float64)
    else:
        nib = np.empty((g, p, n, 4), np.uint8)
        nib[..., 0::2] = words & 0xF
        nib[..., 1::2] = words >> 4
        vals = E2M1[nib]
    vals = vals * np.repeat(np.exp2(scales.astype(np.float64) - 127.0), 8, axis=1)[..., None]
    return vals.transpose(0, 1, 3, 2).reshape(g * 512, n)


B, S, I0, I1, I2, I3, I4, O0, O1, O2, O3, O4, R1, R2, R3, R4 = 4, 2048, 4, 4, 2, 2, 16, 2, 2, 2, 2, 8, 16, 512, 1024, 512
IL, OL = I0 * I1 * I2 * I3, O0 * O1 * O2 * O3
IN, OUT = IL * I4, OL * O4
FMT = "e4m3"


def setup_inputs():
    s = mx_kscale(R4)
    a = mx_kscale(IN)[::I4]
    x = bf(np.random.standard_normal((B, S, IN)) / np.repeat(a, I4))
    t3 = np.random.standard_normal((IL, OL, R4)) * s * a[:, None, None]
    cat = np.swapaxes(t3, 1, 2).reshape(-1, OL)
    t3_words, t3_scales = pack_weight(cat, FMT)
    core4 = bf(np.random.standard_normal((R4, I4, O4, 1)) / np.sqrt(R4 * IN) / s[:, None, None, None])
    bias = bf(np.random.standard_normal(OUT))
    return {"x": x,
            "t3_words": t3_words,
            "t3_scales": t3_scales,
            "core4": core4,
            "bias": bias}


def reference(x, t3_words, t3_scales, core4, bias):
    t3q = unpack_weight(t3_words, t3_scales, FMT).reshape(IL, R4, OL).swapaxes(1, 2).reshape(IL * OL, R4)
    p = t3q @ mxq(f64(core4).reshape(R4, I4 * O4), 0, "e4m3")
    m = p.reshape(IL, OL, I4, O4, 1).transpose(0, 2, 1, 3, 4).reshape(IN, OUT, 1)[:, :, 0]
    y = (mxq(f64(x).reshape(B * S, IN), 1, "e4m3") @ mxq(m, 0, "e4m3")) + f64(bias)
    return y.reshape(B, S, OUT)

@@ -1,0 +1,206 @@
+from contextlib import ExitStack
+
+import concourse.mybir as mybir
+from concourse.masks import make_identity
+
+F32 = mybir.dt.float32
+BF16 = mybir.dt.bfloat16
+I32 = mybir.dt.int32
+U8 = mybir.dt.uint8
+FP8X4 = mybir.dt.float8_e4m3fn_x4
+
+P = 128
+PACK = 4
+TOKENS = 4 * 2048
+K_IN = 1024
+N_OUT = 128
+BOND = 512
+PASSES = K_IN // (P * PACK)
+QUARTERS = 4
+N_A = 16
+N_C = 8
+N_E = 2
+N_O_LEFT = 16
+N_O_LAST = 8
+T3_COLS = QUARTERS * N_O_LEFT
+
+ROWS_PER_PARTITION = TOKENS // P
+UNIT = 4
+UNITS = ROWS_PER_PARTITION // UNIT
+BANK_TILES = 4
+
+FLOPS = 2 * (K_IN * N_OUT) * BOND + 2 * TOKENS * K_IN * N_OUT
+
+
+def tile_linear2mpo_pb_t_e_kernel(tc, x, t3_words, t3_scales, core4, bias, out):
+    nc = tc.nc
+    x_rows = x.flatten_outer_dims().rearrange("(p n) k -> p n k", n=ROWS_PER_PARTITION)
+    out_rows = out.flatten_outer_dims().rearrange("(p n) w -> p n w", n=ROWS_PER_PARTITION)
+
+    with ExitStack() as ctx:
+        ctx.enter_context(tc.manual_schedule())
+        keep = ctx.enter_context(tc.tile_pool(name="keep", bufs=1))
+        x_pool = ctx.enter_context(tc.tile_pool(name="x", bufs=UNITS))
+        y_pool = ctx.enter_context(tc.tile_pool(name="y", bufs=UNITS))
+        stream = ctx.enter_context(tc.tile_pool(name="stream", bufs=3))
+        banks = ctx.enter_context(tc.psum_pool(name="banks", bufs=6))
+        y_banks = ctx.enter_context(tc.psum_pool(name="y_banks", bufs=2))
+
+        core_raw = keep.tile([P, PACK, N_OUT], BF16)
+        nc.scalar.dma_start(out=core_raw[:], in_=core4.rearrange("(p j) i o z -> p j (i o z)", j=PACK))
+        bias_bf16 = keep.tile([P, N_OUT], BF16)
+        nc.scalar.dma_start(out=bias_bf16[:], in_=bias.partition_broadcast(P))
+
+        scales_as_sent = keep.tile([P, QUARTERS * N_A * N_O_LEFT], U8, align_bytes=64)
+        nc.vector.memset(scales_as_sent[:].bitcast(I32), 0)
+        t3_scale_plane = keep.tile([P, N_A, P], U8, align_bytes=64)
+        nc.vector.memset(t3_scale_plane[:].bitcast(I32), 0)
+        t3_codes = keep.tile([P, N_A, P], I32, align_bytes=64)
+        nc.vector.memset(t3_codes[:, :, T3_COLS:P], 0)
+
+        scale_words = t3_scales.bitcast(I32)
+        for quadrant in range(4):
+            nc.sync.dma_start(
+                out=scales_as_sent[32 * quadrant : 32 * quadrant + 4, :].bitcast(I32).rearrange("r (G n) -> r G n", n=4),
+                in_=scale_words[:, 4 * quadrant : 4 * quadrant + 4, :].rearrange("G r n -> r G n"),
+            )
+        code_words = t3_words.rearrange("G p n t -> G p (n t)").bitcast(I32)
+        for h in range(QUARTERS):
+            nc.sync.dma_start(
+                out=t3_codes[:, :, N_O_LEFT * h : N_O_LEFT * (h + 1)],
+                in_=code_words[N_A * h : N_A * (h + 1)].rearrange("a p n -> p a n"),
+            )
+        x_units = []
+        for unit in range(UNITS):
+            x_unit = x_pool.tile([P, UNIT, K_IN], BF16)
+            nc.sync.dma_start(out=x_unit[:], in_=x_rows[:, UNIT * unit : UNIT * (unit + 1), :])
+            x_units.append(x_unit)
+
+        identity = keep.tile([P, P], F32)
+        make_identity(nc, identity[:])
+        bias_f32 = keep.tile([P, N_OUT], F32)
+        nc.gpsimd.tensor_copy(out=bias_f32[:], in_=bias_bf16[:])
+
+        core_grouped = keep.tile([P, N_OUT, PACK], BF16, align_bytes=64)
+        nc.vector.tensor_copy(out=core_grouped[:], in_=core_raw[:].rearrange("p j w -> p w j"))
+        core_codes = keep.tile([P, N_OUT], I32, align_bytes=64)
+        core_scales = keep.tile([P, N_OUT], U8, align_bytes=64)
+        nc.vector.quantize_mx(
+            out=core_codes[:].bitcast(FP8X4),
+            scales=core_scales[:],
+            in_=core_grouped[:].rearrange("p w j -> p (w j)"),
+        )
+        nc.vector.tensor_copy(
+            out=t3_scale_plane[:].bitcast(I32)[:, :, 0 : T3_COLS // 4].rearrange("p a (h n) -> p a h n", n=4),
+            in_=scales_as_sent[:].bitcast(I32).rearrange("p (h a n) -> p a h n", h=QUARTERS, n=4),
+        )
+
+        products = []
+        for bank in range(N_A // BANK_TILES):
+            product = banks.tile([P, BANK_TILES, N_OUT], F32, tag="bank")
+            for slot in range(BANK_TILES):
+                a = BANK_TILES * bank + slot
+                nc.tensor.matmul_mx(
+                    out=product[:, slot, :],
+                    lhsT=t3_codes[:, a, :].bitcast(FP8X4),
+                    lhsT_scale=t3_scale_plane[:, a, :],
+                    rhs=core_codes[:].bitcast(FP8X4),
+                    rhs_scale=core_scales[:],
+                    start=True,
+                    stop=True,
+                )
+            products.append(product)
+        product_sb = keep.tile([P, N_E * N_O_LAST, N_A, N_C], F32)
+        for bank in range(N_A // BANK_TILES):
+            copy_out = nc.scalar.copy if bank % 2 == 0 else nc.vector.tensor_copy
+            copy_out(
+                out=product_sb[:, :, BANK_TILES * bank : BANK_TILES * (bank + 1), :],
+                in_=products[bank][:].rearrange("p a (c s) -> p s a c", c=N_C),
+            )
+        m_banks = []
+        for bank in range(N_O_LAST // 2):
+            m_bank = banks.tile([P, BANK_TILES, P], F32, tag="bank")
+            for slot in range(BANK_TILES):
+                o = 2 * bank + slot // N_E
+                e = slot % N_E
+                nc.tensor.transpose(
+                    m_bank[:, slot, :],
+                    product_sb[:, N_O_LAST * e + o, :, :].rearrange("p a c -> p (a c)"),
+                    identity[:],
+                )
+            m_banks.append(m_bank)
+        m_grouped = keep.tile([P, PASSES, N_OUT, PACK], BF16, align_bytes=64)
+        for bank in range(N_O_LAST // 2):
+            for g in range(PASSES):
+                nc.vector.tensor_copy(
+                    out=m_grouped[:, g, :, :].rearrange("p (O o) (u e) -> p O o u e", o=N_O_LAST, e=N_E)[
+                        :, :, 2 * bank : 2 * bank + 2, :, :
+                    ],
+                    in_=m_banks[bank][:, :, 32 * g : 32 * (g + 1)].rearrange("p (o e) (u O) -> p O o u e", e=N_E, u=2),
+                )
+        m_codes = keep.tile([P, PASSES, N_OUT], I32, align_bytes=64)
+        m_scales = keep.tile([P, PASSES, N_OUT], U8, align_bytes=64)
+        nc.vector.quantize_mx(
+            out=m_codes[:].rearrange("p g w -> p (g w)").bitcast(FP8X4),
+            scales=m_scales[:].rearrange("p g w -> p (g w)"),
+            in_=m_grouped[:].rearrange("p g w t -> p (g w t)"),
+        )
+
+        x_grouped = {}
+        x_codes = {}
+        x_scales = {}
+
+        def transpose_unit(unit):
+            grouped = stream.tile([P, UNIT, K_IN], BF16, align_bytes=64)
+            for j in range(UNIT):
+                words = x_units[unit][:, j, :].bitcast(F32)
+                x_bank = banks.tile([P, QUARTERS, P], F32, tag="bank")
+                for h in range(QUARTERS):
+                    nc.tensor.transpose(x_bank[:, h, :], words[:, P * h : P * (h + 1)], identity[:])
+                nc.scalar.copy(
+                    out=grouped[:, j, :].bitcast(F32).rearrange("p (g r u) -> p g r u", g=PASSES, u=2),
+                    in_=x_bank[:].rearrange("p (g u) r -> p g r u", u=2),
+                )
+            x_grouped[unit] = grouped
+
+        def quantise_unit(unit):
+            codes = stream.tile([P, UNIT * PASSES * P], I32, align_bytes=64)
+            scales = stream.tile([P, UNIT * PASSES * P], U8, align_bytes=64)
+            nc.vector.quantize_mx(
+                out=codes[:].bitcast(FP8X4),
+                scales=scales[:],
+                in_=x_grouped[unit][:].rearrange("p j k -> p (j k)"),
+            )
+            x_codes[unit] = codes
+            x_scales[unit] = scales
+
+        def multiply_unit(unit):
+            y_bank = y_banks.tile([P, UNIT, N_OUT], F32)
+            for j in range(UNIT):
+                for g in range(PASSES):
+                    cols = slice(P * (PASSES * j + g), P * (PASSES * j + g + 1))
+                    nc.tensor.matmul_mx(
+                        out=y_bank[:, j, :],
+                        lhsT=x_codes[unit][:, cols].bitcast(FP8X4),
+                        lhsT_scale=x_scales[unit][:, cols],
+                        rhs=m_codes[:, g, :].bitcast(FP8X4),
+                        rhs_scale=m_scales[:, g, :],
+                        start=(g == 0),
+                        stop=(g == PASSES - 1),
+                    )
+            y_unit = y_pool.tile([P, UNIT, N_OUT], F32)
+            nc.vector.tensor_tensor(
+                out=y_unit[:],
+                in0=y_bank[:],
+                in1=bias_f32[:].unsqueeze(1).to_broadcast([P, UNIT, N_OUT]),
+                op=mybir.AluOpType.add,
+            )
+            nc.sync.dma_start(out=out_rows[:, UNIT * unit : UNIT * (unit + 1), :], in_=y_unit[:])
+
+        for step in range(UNITS + 2):
+            if step < UNITS:
+                transpose_unit(step)
+            if 1 <= step <= UNITS:
+                quantise_unit(step - 1)
+            if step >= 2:
+                multiply_unit(step - 2)

@@ -157,7 +157,8 @@ def tile_linear2mpo_pb_t_e_kernel(tc, x, t3_words, t3_scales, core4, bias, out):
                 x_bank = banks.tile([P, QUARTERS, P], F32, tag="bank")
                 for h in range(QUARTERS):
                     nc.tensor.transpose(x_bank[:, h, :], words[:, P * h : P * (h + 1)], identity[:])
-                nc.scalar.copy(
+                copy_out = nc.vector.tensor_copy if (unit % 2 == 1 and j == UNIT - 1) else nc.scalar.copy
+                copy_out(
                     out=grouped[:, j, :].bitcast(F32).rearrange("p (g r u) -> p g r u", g=PASSES, u=2),
                     in_=x_bank[:].rearrange("p (g u) r -> p g r u", u=2),
                 )
@@ -198,9 +199,9 @@ def tile_linear2mpo_pb_t_e_kernel(tc, x, t3_words, t3_scales, core4, bias, out):
             nc.sync.dma_start(out=out_rows[:, UNIT * unit : UNIT * (unit + 1), :], in_=y_unit[:])
 
         for step in range(UNITS + 2):
-            if step < UNITS:
-                transpose_unit(step)
             if 1 <= step <= UNITS:
                 quantise_unit(step - 1)
+            if step < UNITS:
+                transpose_unit(step)
             if step >= 2:
                 multiply_unit(step - 2)

@@ -48,8 +48,11 @@ def tile_linear2mpo_pb_t_e_kernel(tc, x, t3_words, t3_scales, core4, bias, out):
 
         core_raw = keep.tile([P, PACK, N_OUT], BF16)
         nc.scalar.dma_start(out=core_raw[:], in_=core4.rearrange("(p j) i o z -> p j (i o z)", j=PACK))
-        bias_bf16 = keep.tile([P, N_OUT], BF16)
-        nc.scalar.dma_start(out=bias_bf16[:], in_=bias.partition_broadcast(P))
+        bias_row = keep.tile([P, N_OUT], BF16)
+        nc.gpsimd.memset(bias_row[:], 0.0)
+        nc.scalar.dma_start(out=bias_row[0:1, :], in_=bias.unsqueeze(0))
+        ones = keep.tile([P, P], BF16)
+        nc.gpsimd.memset(ones[:], 1.0)
 
         scales_as_sent = keep.tile([P, QUARTERS * N_A * N_O_LEFT], U8, align_bytes=64)
         nc.vector.memset(scales_as_sent[:].bitcast(I32), 0)
@@ -58,10 +61,10 @@ def tile_linear2mpo_pb_t_e_kernel(tc, x, t3_words, t3_scales, core4, bias, out):
         t3_codes = keep.tile([P, N_A, P], I32, align_bytes=64)
         nc.vector.memset(t3_codes[:, :, T3_COLS:P], 0)
 
-        scale_words = t3_scales.bitcast(I32)
+        scale_words = t3_scales.bitcast(F32)
         for quadrant in range(4):
-            nc.sync.dma_start(
-                out=scales_as_sent[32 * quadrant : 32 * quadrant + 4, :].bitcast(I32).rearrange("r (G n) -> r G n", n=4),
+            nc.gpsimd.dma_start(
+                out=scales_as_sent[32 * quadrant : 32 * quadrant + 4, :].bitcast(F32).rearrange("r (G n) -> r G n", n=4),
                 in_=scale_words[:, 4 * quadrant : 4 * quadrant + 4, :].rearrange("G r n -> r G n"),
             )
         code_words = t3_words.rearrange("G p n t -> G p (n t)").bitcast(I32)
@@ -78,8 +81,10 @@ def tile_linear2mpo_pb_t_e_kernel(tc, x, t3_words, t3_scales, core4, bias, out):
 
         identity = keep.tile([P, P], F32)
         make_identity(nc, identity[:])
+        bias_bank = banks.tile([P, BANK_TILES, N_OUT], F32, tag="bank")
+        nc.tensor.matmul(out=bias_bank[:, 0, :], lhsT=ones[:], rhs=bias_row[:], start=True, stop=True)
         bias_f32 = keep.tile([P, N_OUT], F32)
-        nc.gpsimd.tensor_copy(out=bias_f32[:], in_=bias_bf16[:])
+        nc.scalar.copy(out=bias_f32[:], in_=bias_bank[:, 0, :])
 
         core_grouped = keep.tile([P, N_OUT, PACK], BF16, align_bytes=64)
         nc.vector.tensor_copy(out=core_grouped[:], in_=core_raw[:].rearrange("p j w -> p w j"))

from contextlib import ExitStack

import concourse.mybir as mybir
from concourse.masks import make_identity

F32 = mybir.dt.float32
BF16 = mybir.dt.bfloat16
I32 = mybir.dt.int32
U8 = mybir.dt.uint8
FP8X4 = mybir.dt.float8_e4m3fn_x4

P = 128
PACK = 4
TOKENS = 4 * 2048
K_IN = 1024
N_OUT = 128
BOND = 512
PASSES = K_IN // (P * PACK)
QUARTERS = 4
N_A = 16
N_C = 8
N_E = 2
N_O_LEFT = 16
N_O_LAST = 8
T3_COLS = QUARTERS * N_O_LEFT

ROWS_PER_PARTITION = TOKENS // P
UNIT = 4
UNITS = ROWS_PER_PARTITION // UNIT
BANK_TILES = 4

FLOPS = 2 * (K_IN * N_OUT) * BOND + 2 * TOKENS * K_IN * N_OUT


def tile_linear2mpo_pb_t_e_kernel(tc, x, t3_words, t3_scales, core4, bias, out):
    nc = tc.nc
    x_rows = x.flatten_outer_dims().rearrange("(p n) k -> p n k", n=ROWS_PER_PARTITION)
    out_rows = out.flatten_outer_dims().rearrange("(p n) w -> p n w", n=ROWS_PER_PARTITION)

    with ExitStack() as ctx:
        ctx.enter_context(tc.manual_schedule())
        keep = ctx.enter_context(tc.tile_pool(name="keep", bufs=1))
        x_pool = ctx.enter_context(tc.tile_pool(name="x", bufs=UNITS))
        y_pool = ctx.enter_context(tc.tile_pool(name="y", bufs=UNITS))
        stream = ctx.enter_context(tc.tile_pool(name="stream", bufs=3))
        banks = ctx.enter_context(tc.psum_pool(name="banks", bufs=6))
        y_banks = ctx.enter_context(tc.psum_pool(name="y_banks", bufs=2))

        core_raw = keep.tile([P, PACK, N_OUT], BF16)
        nc.scalar.dma_start(out=core_raw[:], in_=core4.rearrange("(p j) i o z -> p j (i o z)", j=PACK))
        bias_row = keep.tile([P, N_OUT], BF16)
        nc.gpsimd.memset(bias_row[:], 0.0)
        nc.scalar.dma_start(out=bias_row[0:1, :], in_=bias.unsqueeze(0))
        ones = keep.tile([P, P], BF16)
        nc.gpsimd.memset(ones[:], 1.0)

        scales_as_sent = keep.tile([P, QUARTERS * N_A * N_O_LEFT], U8, align_bytes=64)
        nc.vector.memset(scales_as_sent[:].bitcast(I32), 0)
        t3_scale_plane = keep.tile([P, N_A, P], U8, align_bytes=64)
        nc.vector.memset(t3_scale_plane[:].bitcast(I32), 0)
        t3_codes = keep.tile([P, N_A, P], I32, align_bytes=64)
        nc.vector.memset(t3_codes[:, :, T3_COLS:P], 0)

        scale_words = t3_scales.bitcast(F32)
        for quadrant in range(4):
            nc.gpsimd.dma_start(
                out=scales_as_sent[32 * quadrant : 32 * quadrant + 4, :].bitcast(F32).rearrange("r (G n) -> r G n", n=4),
                in_=scale_words[:, 4 * quadrant : 4 * quadrant + 4, :].rearrange("G r n -> r G n"),
            )
        code_words = t3_words.rearrange("G p n t -> G p (n t)").bitcast(I32)
        for h in range(QUARTERS):
            nc.sync.dma_start(
                out=t3_codes[:, :, N_O_LEFT * h : N_O_LEFT * (h + 1)],
                in_=code_words[N_A * h : N_A * (h + 1)].rearrange("a p n -> p a n"),
            )
        x_units = []
        for unit in range(UNITS):
            x_unit = x_pool.tile([P, UNIT, K_IN], BF16)
            nc.sync.dma_start(out=x_unit[:], in_=x_rows[:, UNIT * unit : UNIT * (unit + 1), :])
            x_units.append(x_unit)

        identity = keep.tile([P, P], F32)
        make_identity(nc, identity[:])
        bias_bank = banks.tile([P, BANK_TILES, N_OUT], F32, tag="bank")
        nc.tensor.matmul(out=bias_bank[:, 0, :], lhsT=ones[:], rhs=bias_row[:], start=True, stop=True)
        bias_f32 = keep.tile([P, N_OUT], F32)
        nc.scalar.copy(out=bias_f32[:], in_=bias_bank[:, 0, :])

        core_grouped = keep.tile([P, N_OUT, PACK], BF16, align_bytes=64)
        nc.vector.tensor_copy(out=core_grouped[:], in_=core_raw[:].rearrange("p j w -> p w j"))
        core_codes = keep.tile([P, N_OUT], I32, align_bytes=64)
        core_scales = keep.tile([P, N_OUT], U8, align_bytes=64)
        nc.vector.quantize_mx(
            out=core_codes[:].bitcast(FP8X4),
            scales=core_scales[:],
            in_=core_grouped[:].rearrange("p w j -> p (w j)"),
        )
        nc.vector.tensor_copy(
            out=t3_scale_plane[:].bitcast(I32)[:, :, 0 : T3_COLS // 4].rearrange("p a (h n) -> p a h n", n=4),
            in_=scales_as_sent[:].bitcast(I32).rearrange("p (h a n) -> p a h n", h=QUARTERS, n=4),
        )

        products = []
        for bank in range(N_A // BANK_TILES):
            product = banks.tile([P, BANK_TILES, N_OUT], F32, tag="bank")
            for slot in range(BANK_TILES):
                a = BANK_TILES * bank + slot
                nc.tensor.matmul_mx(
                    out=product[:, slot, :],
                    lhsT=t3_codes[:, a, :].bitcast(FP8X4),
                    lhsT_scale=t3_scale_plane[:, a, :],
                    rhs=core_codes[:].bitcast(FP8X4),
                    rhs_scale=core_scales[:],
                    start=True,
                    stop=True,
                )
            products.append(product)
        product_sb = keep.tile([P, N_E * N_O_LAST, N_A, N_C], F32)
        for bank in range(N_A // BANK_TILES):
            copy_out = nc.scalar.copy if bank % 2 == 0 else nc.vector.tensor_copy
            copy_out(
                out=product_sb[:, :, BANK_TILES * bank : BANK_TILES * (bank + 1), :],
                in_=products[bank][:].rearrange("p a (c s) -> p s a c", c=N_C),
            )
        m_banks = []
        for bank in range(N_O_LAST // 2):
            m_bank = banks.tile([P, BANK_TILES, P], F32, tag="bank")
            for slot in range(BANK_TILES):
                o = 2 * bank + slot // N_E
                e = slot % N_E
                nc.tensor.transpose(
                    m_bank[:, slot, :],
                    product_sb[:, N_O_LAST * e + o, :, :].rearrange("p a c -> p (a c)"),
                    identity[:],
                )
            m_banks.append(m_bank)
        m_grouped = keep.tile([P, PASSES, N_OUT, PACK], BF16, align_bytes=64)
        for bank in range(N_O_LAST // 2):
            for g in range(PASSES):
                nc.vector.tensor_copy(
                    out=m_grouped[:, g, :, :].rearrange("p (O o) (u e) -> p O o u e", o=N_O_LAST, e=N_E)[
                        :, :, 2 * bank : 2 * bank + 2, :, :
                    ],
                    in_=m_banks[bank][:, :, 32 * g : 32 * (g + 1)].rearrange("p (o e) (u O) -> p O o u e", e=N_E, u=2),
                )
        m_codes = keep.tile([P, PASSES, N_OUT], I32, align_bytes=64)
        m_scales = keep.tile([P, PASSES, N_OUT], U8, align_bytes=64)
        nc.vector.quantize_mx(
            out=m_codes[:].rearrange("p g w -> p (g w)").bitcast(FP8X4),
            scales=m_scales[:].rearrange("p g w -> p (g w)"),
            in_=m_grouped[:].rearrange("p g w t -> p (g w t)"),
        )

        x_grouped = {}
        x_codes = {}
        x_scales = {}

        def transpose_unit(unit):
            grouped = stream.tile([P, UNIT, K_IN], BF16, align_bytes=64)
            for j in range(UNIT):
                words = x_units[unit][:, j, :].bitcast(F32)
                x_bank = banks.tile([P, QUARTERS, P], F32, tag="bank")
                for h in range(QUARTERS):
                    nc.tensor.transpose(x_bank[:, h, :], words[:, P * h : P * (h + 1)], identity[:])
                copy_out = nc.vector.tensor_copy if (unit % 2 == 1 and j == UNIT - 1) else nc.scalar.copy
                copy_out(
                    out=grouped[:, j, :].bitcast(F32).rearrange("p (g r u) -> p g r u", g=PASSES, u=2),
                    in_=x_bank[:].rearrange("p (g u) r -> p g r u", u=2),
                )
            x_grouped[unit] = grouped

        def quantise_unit(unit):
            codes = stream.tile([P, UNIT * PASSES * P], I32, align_bytes=64)
            scales = stream.tile([P, UNIT * PASSES * P], U8, align_bytes=64)
            nc.vector.quantize_mx(
                out=codes[:].bitcast(FP8X4),
                scales=scales[:],
                in_=x_grouped[unit][:].rearrange("p j k -> p (j k)"),
            )
            x_codes[unit] = codes
            x_scales[unit] = scales

        def multiply_unit(unit):
            y_bank = y_banks.tile([P, UNIT, N_OUT], F32)
            for j in range(UNIT):
                for g in range(PASSES):
                    cols = slice(P * (PASSES * j + g), P * (PASSES * j + g + 1))
                    nc.tensor.matmul_mx(
                        out=y_bank[:, j, :],
                        lhsT=x_codes[unit][:, cols].bitcast(FP8X4),
                        lhsT_scale=x_scales[unit][:, cols],
                        rhs=m_codes[:, g, :].bitcast(FP8X4),
                        rhs_scale=m_scales[:, g, :],
                        start=(g == 0),
                        stop=(g == PASSES - 1),
                    )
            y_unit = y_pool.tile([P, UNIT, N_OUT], F32)
            nc.vector.tensor_tensor(
                out=y_unit[:],
                in0=y_bank[:],
                in1=bias_f32[:].unsqueeze(1).to_broadcast([P, UNIT, N_OUT]),
                op=mybir.AluOpType.add,
            )
            nc.sync.dma_start(out=out_rows[:, UNIT * unit : UNIT * (unit + 1), :], in_=y_unit[:])

        for step in range(UNITS + 2):
            if 1 <= step <= UNITS:
                quantise_unit(step - 1)
            if step < UNITS:
                transpose_unit(step)
            if step >= 2:
                multiply_unit(step - 2)
